import numpy as np
import ml_dtypes


def mxq(x, axis, fmt="e4m3"):
    dtype, down = {"e4m3": (ml_dtypes.float8_e4m3fn, 7), "e5m2": (ml_dtypes.float8_e5m2, 14)}[fmt]
    v = np.moveaxis(np.asarray(x, np.float32).astype(ml_dtypes.bfloat16).astype(np.float64), axis, -1)
    blocks = v.reshape(v.shape[:-1] + (-1, 32))
    amax = np.abs(blocks).max(-1, keepdims=True)
    byte = np.maximum(np.where(amax > 0, np.frexp(amax)[1] - 1 + 127, 0) - down, 1)
    scale = np.exp2(byte - 127.0)
    codes = (blocks / scale).astype(np.float32).astype(dtype).astype(np.float64)
    return np.moveaxis((codes * scale).reshape(v.shape), -1, axis)


WIDE = False


def mx_kscale(k):
    if not WIDE:
        return np.ones(k)
    levels = np.array([10, -10, 5, -5, 0])
    a = np.random.permutation(np.resize(levels, k // 512 * 4)).reshape(k // 512, 4)
    idx = np.arange(k)
    return np.exp2(a[idx // 512, idx % 128 // 32])


BF16 = ml_dtypes.bfloat16


def bf(x):
    return np.asarray(x, np.float32).astype(BF16)


def f64(x):
    return np.asarray(x).astype(np.float64)


B, L, D, F, K = 1024, 8, 512, 512, 16
EPS = 1e-12


def silu(v):
    return v / (1.0 + np.exp(-v))


def l2norm(t, axis):
    n = np.sqrt((t * t).sum(axis=axis, keepdims=True))
    return t / np.maximum(n, EPS)


def mix_draw(rows, cols):
    return np.random.standard_normal((L, rows, cols)) * np.sqrt(np.e / K) * np.exp(0.5 * np.random.standard_normal((L, 1, cols)))


def hidden_draw():
    return silu(3.0 * np.random.standard_normal((B, L, F))) * np.random.standard_normal((B, L, F)) * 3.0 / np.sqrt(D)


def setup_inputs():
    t = mx_kscale(F)
    g = np.sqrt(np.mean(1.0 / t**2))
    return {"h": bf(hidden_draw() * t * g),
            "w_down_mix": bf(mix_draw(F, D) / t[:, None])}


def reference(h, w_down_mix):
    wd = l2norm(f64(w_down_mix), 1)
    y = mxq(f64(h).transpose(1, 0, 2), 2, "e4m3") @ mxq(wd, 1, "e4m3")
    return l2norm(y, -1).transpose(1, 0, 2)

@@ -1,0 +1,224 @@
+from contextlib import ExitStack
+
+import concourse.mybir as mybir
+from concourse.masks import make_identity
+
+F32 = mybir.dt.float32
+BF16 = mybir.dt.bfloat16
+U32 = mybir.dt.uint32
+U8 = mybir.dt.uint8
+FP8X4 = mybir.dt.float8_e4m3fn_x4
+ACT = mybir.ActivationFunctionType
+ALU = mybir.AluOpType
+
+P = 128
+BATCH = 1024
+TOKENS = 8
+HIDDEN = 512
+FEATURES = 512
+PACK = 4
+EPS = 1e-12
+
+BATCH_TILES = BATCH // P
+COLUMN_BLOCKS = FEATURES // P
+GROUP = 4
+GROUPS = BATCH_TILES * TOKENS // GROUP
+GROUPS_PER_TILE = TOKENS // GROUP
+
+FLOPS = 2 * BATCH * TOKENS * HIDDEN * FEATURES
+
+
+def tile_npertokenswishglu_basis_pb_t_kernel(tc, h, w_down_mix, out):
+    nc = tc.nc
+    with ExitStack() as ctx:
+        ctx.enter_context(tc.manual_schedule())
+        const = ctx.enter_context(tc.tile_pool(name="const", bufs=1))
+        raw = ctx.enter_context(tc.tile_pool(name="raw", bufs=1))
+        keep = ctx.enter_context(tc.tile_pool(name="keep", bufs=1))
+        stage = ctx.enter_context(tc.tile_pool(name="stage", bufs=2))
+        small = ctx.enter_context(tc.tile_pool(name="small", bufs=3))
+        results = ctx.enter_context(tc.tile_pool(name="results", bufs=4))
+
+        w_raw = []
+        h_raw = []
+        for i in range(TOKENS):
+            w_tile = raw.tile([P, PACK, FEATURES], BF16, name="w_raw%d" % i)
+            nc.sync.dma_start(
+                out=w_tile[:].rearrange("q (u e) j -> q u e j", u=2),
+                in_=w_down_mix[i].rearrange("(u q e) j -> q u e j", u=2, e=2),
+            )
+            w_raw.append(w_tile)
+            h_tile = raw.tile([P, TOKENS * HIDDEN], BF16, name="h_raw%d" % i)
+            nc.sync.dma_start(
+                out=h_tile[:], in_=h[i * P : (i + 1) * P].rearrange("b l f -> b (l f)")
+            )
+            h_raw.append(h_tile)
+
+        ident_bf16 = const.tile([P, P], BF16)
+        make_identity(nc, ident_bf16[:])
+        ident_f32 = const.tile([P, P], F32)
+        make_identity(nc, ident_f32[:])
+
+        one = const.tile([P, 1], F32)
+        nc.vector.memset(one[:], 1.0)
+        one_root = const.tile([P, 1], F32)
+        nc.scalar.activation(out=one_root[:], in_=one[:], func=ACT.Sqrt)
+
+        w_codes = [keep.tile([P, FEATURES], U32, name="w_codes%d" % l, align_bytes=64) for l in range(TOKENS)]
+        w_scales = [keep.tile([P, FEATURES], U8, name="w_scales%d" % l, align_bytes=64) for l in range(TOKENS)]
+        h_codes = [keep.tile([P, TOKENS * P], U32, name="h_codes%d" % t, align_bytes=64) for t in range(BATCH_TILES)]
+        h_scales = [keep.tile([P, TOKENS * P], U8, name="h_scales%d" % t, align_bytes=64) for t in range(BATCH_TILES)]
+
+        def sum_of_squares(values, total):
+            squares = stage.tile([P, HIDDEN], BF16, name="squares", bufs=4)
+            nc.scalar.activation(out=squares[:], in_=values, func=ACT.Square, accum_out=total)
+
+        def clamp_and_invert(totals, width):
+            clamped = small.tile([P, width], F32, name="clamped")
+            nc.vector.tensor_scalar_max(out=clamped[:], in0=totals[:], scalar1=EPS * EPS)
+            inverse = small.tile([P, width], F32, name="inverse")
+            nc.vector.reciprocal(out=inverse[:], in_=clamped[:])
+            return inverse
+
+        def root(inverse, width):
+            scale = small.tile([P, width], F32, name="scale")
+            nc.scalar.activation(out=scale[:], in_=inverse[:], func=ACT.Sqrt)
+            return scale
+
+        with tc.psum_pool(name="prep_psum", bufs=2) as prep_psum:
+            w_scale = {}
+            w_inverse = {}
+            w_spread = {}
+            nd = {}
+            h_grouped = {}
+            h_flipped = {}
+            for i in range(TOKENS + 1):
+                if i < TOKENS:
+                    w_flipped = []
+                    for half in range(2):
+                        flipped = prep_psum.tile([P, 2, PACK, P], BF16, name="w_flipped", bufs=2)
+                        for c in range(2):
+                            block = 2 * half + c
+                            for t in range(PACK):
+                                nc.tensor.transpose(
+                                    out=flipped[:, c, t, :],
+                                    in_=w_raw[i][:, t, block * P : (block + 1) * P],
+                                    identity=ident_bf16[:],
+                                )
+                        w_flipped.append(flipped)
+                    h_words = h_raw[i][:].bitcast(F32)
+                    h_flipped[i] = []
+                    for pair in range(TOKENS // 2):
+                        flipped = prep_psum.tile([P, 2, 2, P], F32, name="h_flipped", bufs=4)
+                        for c in range(2):
+                            for u in range(2):
+                                first = (2 * pair + c) * (HIDDEN // 2) + u * P
+                                nc.tensor.transpose(
+                                    out=flipped[:, c, u, :],
+                                    in_=h_words[:, first : first + P],
+                                    identity=ident_f32[:],
+                                )
+                        h_flipped[i].append(flipped)
+                if i >= 1:
+                    w_spread[i - 1] = prep_psum.tile([P, FEATURES], F32, name="w_spread", bufs=2)
+                    for block in range(COLUMN_BLOCKS):
+                        nc.tensor.matmul(
+                            out=w_spread[i - 1][:, block * P : (block + 1) * P],
+                            lhsT=w_scale[i - 1][:, block : block + 1].to_broadcast([P, P]),
+                            rhs=ident_f32[:],
+                            start=True,
+                            stop=True,
+                        )
+                if i < TOKENS:
+                    w_totals = small.tile([P, COLUMN_BLOCKS], F32, name="w_totals")
+                    for block in range(COLUMN_BLOCKS):
+                        sum_of_squares(
+                            w_flipped[block // 2][:, block % 2].rearrange("j t q -> j (t q)"),
+                            w_totals[:, block : block + 1],
+                        )
+                if i >= 1:
+                    for half in range(2):
+                        nc.vector.quantize_mx(
+                            out=h_codes[i - 1][:, half * 512 : (half + 1) * 512].bitcast(FP8X4),
+                            scales=h_scales[i - 1][:, half * 512 : (half + 1) * 512],
+                            in_=h_grouped[i - 1][:, half * 2048 : (half + 1) * 2048],
+                        )
+                    nd[i - 1] = stage.tile([P, FEATURES, PACK], BF16, name="nd", align_bytes=64)
+                    nc.vector.tensor_tensor(
+                        out=nd[i - 1][:],
+                        in0=w_raw[i - 1][:].rearrange("q t j -> q j t"),
+                        in1=w_spread[i - 1][:].unsqueeze(2).to_broadcast([P, FEATURES, PACK]),
+                        op=ALU.mult,
+                    )
+                if i < TOKENS:
+                    h_grouped[i] = stage.tile([P, TOKENS * P * PACK], BF16, name="h_grouped", align_bytes=64)
+                    grouped_words = h_grouped[i][:].bitcast(F32)
+
+                    def regroup(copy, pair):
+                        copy(
+                            out=grouped_words[:, pair * 512 : (pair + 1) * 512].rearrange(
+                                "q (c b u) -> q c b u", c=2, u=2
+                            ),
+                            in_=h_flipped[i][pair][:].rearrange("q c u b -> q c b u"),
+                        )
+
+                    for pair in range(3):
+                        regroup(nc.scalar.copy, pair)
+                    w_inverse[i] = clamp_and_invert(w_totals, COLUMN_BLOCKS)
+                    regroup(nc.vector.tensor_copy, 3)
+                    w_scale[i] = root(w_inverse[i], COLUMN_BLOCKS)
+                if i >= 1:
+                    nc.vector.quantize_mx(
+                        out=w_codes[i - 1][:].bitcast(FP8X4),
+                        scales=w_scales[i - 1][:],
+                        in_=nd[i - 1][:].rearrange("q j t -> q (j t)"),
+                    )
+
+        with tc.psum_pool(name="y_psum", bufs=8, reuse_waits="tile") as y_psum:
+            y = {}
+            y_totals = {}
+            y_inverse = {}
+            y_scale = {}
+            normed = {}
+
+            def scale_rows(g, k):
+                nc.vector.tensor_scalar_mul(
+                    out=normed[g][:, k, :], in0=y[g][k][:], scalar1=y_scale[g][:, k : k + 1]
+                )
+
+            for g in range(GROUPS + 1):
+                if g < GROUPS:
+                    tile_index = g // GROUPS_PER_TILE
+                    y[g] = []
+                    for k in range(GROUP):
+                        l = (g % GROUPS_PER_TILE) * GROUP + k
+                        acc = y_psum.tile([P, FEATURES], F32, name="y")
+                        nc.tensor.matmul_mx(
+                            out=acc[:],
+                            lhsT=h_codes[tile_index][:, l * P : (l + 1) * P].bitcast(FP8X4),
+                            lhsT_scale=h_scales[tile_index][:, l * P : (l + 1) * P],
+                            rhs=w_codes[l][:].bitcast(FP8X4),
+                            rhs_scale=w_scales[l][:],
+                            start=True,
+                            stop=True,
+                        )
+                        y[g].append(acc)
+                    y_totals[g] = small.tile([P, GROUP], F32, name="y_totals")
+                    sum_of_squares(y[g][0][:], y_totals[g][:, 0:1])
+                if g >= 1:
+                    y_scale[g - 1] = root(y_inverse[g - 1], GROUP)
+                    normed[g - 1] = results.tile([P, GROUP, FEATURES], F32, name="normed")
+                    for k in range(GROUP - 1):
+                        scale_rows(g - 1, k)
+                if g < GROUPS:
+                    for k in range(1, GROUP):
+                        sum_of_squares(y[g][k][:], y_totals[g][:, k : k + 1])
+                    y_inverse[g] = clamp_and_invert(y_totals[g], GROUP)
+                if g >= 1:
+                    scale_rows(g - 1, GROUP - 1)
+                    done_tile = (g - 1) // GROUPS_PER_TILE
+                    first_token = ((g - 1) % GROUPS_PER_TILE) * GROUP
+                    nc.sync.dma_start(
+                        out=out[done_tile * P : (done_tile + 1) * P, first_token : first_token + GROUP, :],
+                        in_=normed[g - 1][:],
+                    )

@@ -24,6 +24,7 @@ COLUMN_BLOCKS = FEATURES // P
 GROUP = 4
 GROUPS = BATCH_TILES * TOKENS // GROUP
 GROUPS_PER_TILE = TOKENS // GROUP
+TILES_REGROUPED_BY_VECTOR = 2
 
 FLOPS = 2 * BATCH * TOKENS * HIDDEN * FEATURES
 
@@ -86,93 +87,116 @@ def tile_npertokenswishglu_basis_pb_t_kernel(tc, h, w_down_mix, out):
             return scale
 
         with tc.psum_pool(name="prep_psum", bufs=2) as prep_psum:
-            w_scale = {}
+            w_flipped = {}
+            w_totals = {}
             w_inverse = {}
+            w_scale = {}
             w_spread = {}
             nd = {}
             h_grouped = {}
             h_flipped = {}
-            for i in range(TOKENS + 1):
-                if i < TOKENS:
-                    w_flipped = []
-                    for half in range(2):
-                        flipped = prep_psum.tile([P, 2, PACK, P], BF16, name="w_flipped", bufs=2)
-                        for c in range(2):
-                            block = 2 * half + c
-                            for t in range(PACK):
-                                nc.tensor.transpose(
-                                    out=flipped[:, c, t, :],
-                                    in_=w_raw[i][:, t, block * P : (block + 1) * P],
-                                    identity=ident_bf16[:],
-                                )
-                        w_flipped.append(flipped)
-                    h_words = h_raw[i][:].bitcast(F32)
-                    h_flipped[i] = []
-                    for pair in range(TOKENS // 2):
-                        flipped = prep_psum.tile([P, 2, 2, P], F32, name="h_flipped", bufs=4)
-                        for c in range(2):
-                            for u in range(2):
-                                first = (2 * pair + c) * (HIDDEN // 2) + u * P
-                                nc.tensor.transpose(
-                                    out=flipped[:, c, u, :],
-                                    in_=h_words[:, first : first + P],
-                                    identity=ident_f32[:],
-                                )
-                        h_flipped[i].append(flipped)
-                if i >= 1:
-                    w_spread[i - 1] = prep_psum.tile([P, FEATURES], F32, name="w_spread", bufs=2)
-                    for block in range(COLUMN_BLOCKS):
-                        nc.tensor.matmul(
-                            out=w_spread[i - 1][:, block * P : (block + 1) * P],
-                            lhsT=w_scale[i - 1][:, block : block + 1].to_broadcast([P, P]),
-                            rhs=ident_f32[:],
-                            start=True,
-                            stop=True,
-                        )
-                if i < TOKENS:
-                    w_totals = small.tile([P, COLUMN_BLOCKS], F32, name="w_totals")
-                    for block in range(COLUMN_BLOCKS):
-                        sum_of_squares(
-                            w_flipped[block // 2][:, block % 2].rearrange("j t q -> j (t q)"),
-                            w_totals[:, block : block + 1],
-                        )
-                if i >= 1:
-                    for half in range(2):
-                        nc.vector.quantize_mx(
-                            out=h_codes[i - 1][:, half * 512 : (half + 1) * 512].bitcast(FP8X4),
-                            scales=h_scales[i - 1][:, half * 512 : (half + 1) * 512],
-                            in_=h_grouped[i - 1][:, half * 2048 : (half + 1) * 2048],
-                        )
-                    nd[i - 1] = stage.tile([P, FEATURES, PACK], BF16, name="nd", align_bytes=64)
-                    nc.vector.tensor_tensor(
-                        out=nd[i - 1][:],
-                        in0=w_raw[i - 1][:].rearrange("q t j -> q j t"),
-                        in1=w_spread[i - 1][:].unsqueeze(2).to_broadcast([P, FEATURES, PACK]),
-                        op=ALU.mult,
+
+            def flip_weight(i):
+                for half in range(2):
+                    w_flipped[i, half] = prep_psum.tile([P, 2, PACK, P], BF16, name="w_flipped", bufs=2)
+                    for k in range(2):
+                        block = 2 * half + k
+                        for t in range(PACK):
+                            nc.tensor.transpose(
+                                out=w_flipped[i, half][:, k, t, :],
+                                in_=w_raw[i][:, t, block * P : (block + 1) * P],
+                                identity=ident_bf16[:],
+                            )
+
+            def flip_h(i):
+                h_words = h_raw[i][:].bitcast(F32)
+                for pair in range(TOKENS // 2):
+                    h_flipped[i, pair] = prep_psum.tile([P, 2, 2, P], F32, name="h_flipped", bufs=4)
+                    for k in range(2):
+                        for u in range(2):
+                            first = (2 * pair + k) * (HIDDEN // 2) + u * P
+                            nc.tensor.transpose(
+                                out=h_flipped[i, pair][:, k, u, :],
+                                in_=h_words[:, first : first + P],
+                                identity=ident_f32[:],
+                            )
+
+            def spread_weight_scale(i):
+                w_spread[i] = prep_psum.tile([P, FEATURES], F32, name="w_spread", bufs=2)
+                for block in range(COLUMN_BLOCKS):
+                    nc.tensor.matmul(
+                        out=w_spread[i][:, block * P : (block + 1) * P],
+                        lhsT=w_scale[i][:, block : block + 1].to_broadcast([P, P]),
+                        rhs=ident_f32[:],
+                        start=True,
+                        stop=True,
                     )
-                if i < TOKENS:
-                    h_grouped[i] = stage.tile([P, TOKENS * P * PACK], BF16, name="h_grouped", align_bytes=64)
-                    grouped_words = h_grouped[i][:].bitcast(F32)
 
-                    def regroup(copy, pair):
-                        copy(
-                            out=grouped_words[:, pair * 512 : (pair + 1) * 512].rearrange(
-                                "q (c b u) -> q c b u", c=2, u=2
-                            ),
-                            in_=h_flipped[i][pair][:].rearrange("q c u b -> q c b u"),
-                        )
+            def weight_column_sums(i):
+                w_totals[i] = small.tile([P, COLUMN_BLOCKS], F32, name="w_totals")
+                for block in range(COLUMN_BLOCKS):
+                    sum_of_squares(
+                        w_flipped[i, block // 2][:, block % 2].rearrange("j t q -> j (t q)"),
+                        w_totals[i][:, block : block + 1],
+                    )
 
-                    for pair in range(3):
-                        regroup(nc.scalar.copy, pair)
-                    w_inverse[i] = clamp_and_invert(w_totals, COLUMN_BLOCKS)
-                    regroup(nc.vector.tensor_copy, 3)
-                    w_scale[i] = root(w_inverse[i], COLUMN_BLOCKS)
-                if i >= 1:
+            def regroup_h(i):
+                h_grouped[i] = stage.tile([P, TOKENS * P * PACK], BF16, name="h_grouped", align_bytes=64, bufs=3)
+                grouped_words = h_grouped[i][:].bitcast(F32)
+                copy = nc.vector.tensor_copy if i < TILES_REGROUPED_BY_VECTOR else nc.scalar.copy
+                for pair in range(TOKENS // 2):
+                    copy(
+                        out=grouped_words[:, pair * 512 : (pair + 1) * 512].rearrange(
+                            "q (k b u) -> q k b u", k=2, u=2
+                        ),
+                        in_=h_flipped[i, pair][:].rearrange("q k u b -> q k b u"),
+                    )
+
+            def quantise_h(i):
+                for half in range(2):
                     nc.vector.quantize_mx(
-                        out=w_codes[i - 1][:].bitcast(FP8X4),
-                        scales=w_scales[i - 1][:],
-                        in_=nd[i - 1][:].rearrange("q j t -> q (j t)"),
+                        out=h_codes[i][:, half * 512 : (half + 1) * 512].bitcast(FP8X4),
+                        scales=h_scales[i][:, half * 512 : (half + 1) * 512],
+                        in_=h_grouped[i][:, half * 2048 : (half + 1) * 2048],
                     )
+
+            def normalise_weight(i):
+                nd[i] = stage.tile([P, FEATURES, PACK], BF16, name="nd", align_bytes=64)
+                nc.vector.tensor_tensor(
+                    out=nd[i][:],
+                    in0=w_raw[i][:].rearrange("q t j -> q j t"),
+                    in1=w_spread[i][:].unsqueeze(2).to_broadcast([P, FEATURES, PACK]),
+                    op=ALU.mult,
+                )
+
+            def quantise_weight(i):
+                nc.vector.quantize_mx(
+                    out=w_codes[i][:].bitcast(FP8X4),
+                    scales=w_scales[i][:],
+                    in_=nd[i][:].rearrange("q j t -> q (j t)"),
+                )
+
+            for n in range(TOKENS + 2):
+                first = n
+                second = n - 1
+                third = n - 2
+                if first < TOKENS:
+                    flip_weight(first)
+                if 0 <= third:
+                    spread_weight_scale(third)
+                if first < TOKENS:
+                    flip_h(first)
+                    weight_column_sums(first)
+                if 0 <= second < TOKENS:
+                    w_inverse[second] = clamp_and_invert(w_totals[second], COLUMN_BLOCKS)
+                    w_scale[second] = root(w_inverse[second], COLUMN_BLOCKS)
+                    quantise_h(second)
+                if 0 <= third:
+                    normalise_weight(third)
+                if first < TOKENS:
+                    regroup_h(first)
+                if 0 <= third:
+                    quantise_weight(third)
 
         with tc.psum_pool(name="y_psum", bufs=8, reuse_waits="tile") as y_psum:
             y = {}

@@ -96,41 +96,38 @@ def tile_npertokenswishglu_basis_pb_t_kernel(tc, h, w_down_mix, out):
             h_grouped = {}
             h_flipped = {}
 
-            def flip_weight(i):
-                for half in range(2):
-                    w_flipped[i, half] = prep_psum.tile([P, 2, PACK, P], BF16, name="w_flipped", bufs=2)
-                    for k in range(2):
-                        block = 2 * half + k
-                        for t in range(PACK):
-                            nc.tensor.transpose(
-                                out=w_flipped[i, half][:, k, t, :],
-                                in_=w_raw[i][:, t, block * P : (block + 1) * P],
-                                identity=ident_bf16[:],
-                            )
-
-            def flip_h(i):
-                h_words = h_raw[i][:].bitcast(F32)
-                for pair in range(TOKENS // 2):
-                    h_flipped[i, pair] = prep_psum.tile([P, 2, 2, P], F32, name="h_flipped", bufs=4)
-                    for k in range(2):
-                        for u in range(2):
-                            first = (2 * pair + k) * (HIDDEN // 2) + u * P
-                            nc.tensor.transpose(
-                                out=h_flipped[i, pair][:, k, u, :],
-                                in_=h_words[:, first : first + P],
-                                identity=ident_f32[:],
-                            )
-
-            def spread_weight_scale(i):
-                w_spread[i] = prep_psum.tile([P, FEATURES], F32, name="w_spread", bufs=2)
-                for block in range(COLUMN_BLOCKS):
-                    nc.tensor.matmul(
-                        out=w_spread[i][:, block * P : (block + 1) * P],
-                        lhsT=w_scale[i][:, block : block + 1].to_broadcast([P, P]),
-                        rhs=ident_f32[:],
-                        start=True,
-                        stop=True,
+            def flip_weight(i, block):
+                if block % 2 == 0:
+                    w_flipped[i, block // 2] = prep_psum.tile([P, 2, PACK, P], BF16, name="w_flipped", bufs=2)
+                for t in range(PACK):
+                    nc.tensor.transpose(
+                        out=w_flipped[i, block // 2][:, block % 2, t, :],
+                        in_=w_raw[i][:, t, block * P : (block + 1) * P],
+                        identity=ident_bf16[:],
                     )
+
+            def flip_h(i, pair):
+                h_words = h_raw[i][:].bitcast(F32)
+                h_flipped[i, pair] = prep_psum.tile([P, 2, 2, P], F32, name="h_flipped", bufs=4)
+                for k in range(2):
+                    for u in range(2):
+                        start_word = (2 * pair + k) * (HIDDEN // 2) + u * P
+                        nc.tensor.transpose(
+                            out=h_flipped[i, pair][:, k, u, :],
+                            in_=h_words[:, start_word : start_word + P],
+                            identity=ident_f32[:],
+                        )
+
+            def spread_weight_scale(i, block):
+                if block == 0:
+                    w_spread[i] = prep_psum.tile([P, FEATURES], F32, name="w_spread", bufs=2)
+                nc.tensor.matmul(
+                    out=w_spread[i][:, block * P : (block + 1) * P],
+                    lhsT=w_scale[i][:, block : block + 1].to_broadcast([P, P]),
+                    rhs=ident_f32[:],
+                    start=True,
+                    stop=True,
+                )
 
             def weight_column_sums(i):
                 w_totals[i] = small.tile([P, COLUMN_BLOCKS], F32, name="w_totals")
@@ -180,12 +177,14 @@ def tile_npertokenswishglu_basis_pb_t_kernel(tc, h, w_down_mix, out):
                 first = n
                 second = n - 1
                 third = n - 2
+                for quarter in range(COLUMN_BLOCKS):
+                    if first < TOKENS:
+                        flip_weight(first, quarter)
+                    if 0 <= third:
+                        spread_weight_scale(third, quarter)
+                    if first < TOKENS:
+                        flip_h(first, quarter)
                 if first < TOKENS:
-                    flip_weight(first)
-                if 0 <= third:
-                    spread_weight_scale(third)
-                if first < TOKENS:
-                    flip_h(first)
                     weight_column_sums(first)
                 if 0 <= second < TOKENS:
                     w_inverse[second] = clamp_and_invert(w_totals[second], COLUMN_BLOCKS)

@@ -63,7 +63,7 @@ def tile_npertokenswishglu_basis_pb_t_kernel(tc, h, w_down_mix, out):
         one = const.tile([P, 1], F32)
         nc.vector.memset(one[:], 1.0)
         one_root = const.tile([P, 1], F32)
-        nc.scalar.activation(out=one_root[:], in_=one[:], func=ACT.Sqrt)
+        nc.scalar.activation(out=one_root[:], in_=one[:], func=ACT.Abs_reciprocal_sqrt)
 
         w_codes = [keep.tile([P, FEATURES], U32, name="w_codes%d" % l, align_bytes=64) for l in range(TOKENS)]
         w_scales = [keep.tile([P, FEATURES], U8, name="w_scales%d" % l, align_bytes=64) for l in range(TOKENS)]
@@ -77,13 +77,11 @@ def tile_npertokenswishglu_basis_pb_t_kernel(tc, h, w_down_mix, out):
         def clamp_and_invert(totals, width):
             clamped = small.tile([P, width], F32, name="clamped")
             nc.vector.tensor_scalar_max(out=clamped[:], in0=totals[:], scalar1=EPS * EPS)
-            inverse = small.tile([P, width], F32, name="inverse")
-            nc.vector.reciprocal(out=inverse[:], in_=clamped[:])
-            return inverse
+            return clamped
 
-        def root(inverse, width):
+        def root(clamped, width):
             scale = small.tile([P, width], F32, name="scale")
-            nc.scalar.activation(out=scale[:], in_=inverse[:], func=ACT.Sqrt)
+            nc.scalar.activation(out=scale[:], in_=clamped[:], func=ACT.Abs_reciprocal_sqrt)
             return scale
 
         with tc.psum_pool(name="prep_psum", bufs=2) as prep_psum:
@@ -96,38 +94,41 @@ def tile_npertokenswishglu_basis_pb_t_kernel(tc, h, w_down_mix, out):
             h_grouped = {}
             h_flipped = {}
 
-            def flip_weight(i, block):
-                if block % 2 == 0:
-                    w_flipped[i, block // 2] = prep_psum.tile([P, 2, PACK, P], BF16, name="w_flipped", bufs=2)
-                for t in range(PACK):
-                    nc.tensor.transpose(
-                        out=w_flipped[i, block // 2][:, block % 2, t, :],
-                        in_=w_raw[i][:, t, block * P : (block + 1) * P],
-                        identity=ident_bf16[:],
-                    )
+            def flip_weight(i):
+                for half in range(2):
+                    w_flipped[i, half] = prep_psum.tile([P, 2, PACK, P], BF16, name="w_flipped", bufs=2)
+                    for k in range(2):
+                        block = 2 * half + k
+                        for t in range(PACK):
+                            nc.tensor.transpose(
+                                out=w_flipped[i, half][:, k, t, :],
+                                in_=w_raw[i][:, t, block * P : (block + 1) * P],
+                                identity=ident_bf16[:],
+                            )
 
-            def flip_h(i, pair):
+            def flip_h(i):
                 h_words = h_raw[i][:].bitcast(F32)
-                h_flipped[i, pair] = prep_psum.tile([P, 2, 2, P], F32, name="h_flipped", bufs=4)
-                for k in range(2):
-                    for u in range(2):
-                        start_word = (2 * pair + k) * (HIDDEN // 2) + u * P
-                        nc.tensor.transpose(
-                            out=h_flipped[i, pair][:, k, u, :],
-                            in_=h_words[:, start_word : start_word + P],
-                            identity=ident_f32[:],
-                        )
+                for pair in range(TOKENS // 2):
+                    h_flipped[i, pair] = prep_psum.tile([P, 2, 2, P], F32, name="h_flipped", bufs=4)
+                    for k in range(2):
+                        for u in range(2):
+                            first = (2 * pair + k) * (HIDDEN // 2) + u * P
+                            nc.tensor.transpose(
+                                out=h_flipped[i, pair][:, k, u, :],
+                                in_=h_words[:, first : first + P],
+                                identity=ident_f32[:],
+                            )
 
-            def spread_weight_scale(i, block):
-                if block == 0:
-                    w_spread[i] = prep_psum.tile([P, FEATURES], F32, name="w_spread", bufs=2)
-                nc.tensor.matmul(
-                    out=w_spread[i][:, block * P : (block + 1) * P],
-                    lhsT=w_scale[i][:, block : block + 1].to_broadcast([P, P]),
-                    rhs=ident_f32[:],
-                    start=True,
-                    stop=True,
-                )
+            def spread_weight_scale(i):
+                w_spread[i] = prep_psum.tile([P, FEATURES], F32, name="w_spread", bufs=2)
+                for block in range(COLUMN_BLOCKS):
+                    nc.tensor.matmul(
+                        out=w_spread[i][:, block * P : (block + 1) * P],
+                        lhsT=w_scale[i][:, block : block + 1].to_broadcast([P, P]),
+                        rhs=ident_f32[:],
+                        start=True,
+                        stop=True,
+                    )
 
             def weight_column_sums(i):
                 w_totals[i] = small.tile([P, COLUMN_BLOCKS], F32, name="w_totals")
@@ -177,14 +178,12 @@ def tile_npertokenswishglu_basis_pb_t_kernel(tc, h, w_down_mix, out):
                 first = n
                 second = n - 1
                 third = n - 2
-                for quarter in range(COLUMN_BLOCKS):
-                    if first < TOKENS:
-                        flip_weight(first, quarter)
-                    if 0 <= third:
-                        spread_weight_scale(third, quarter)
-                    if first < TOKENS:
-                        flip_h(first, quarter)
                 if first < TOKENS:
+                    flip_weight(first)
+                if 0 <= third:
+                    spread_weight_scale(third)
+                if first < TOKENS:
+                    flip_h(first)
                     weight_column_sums(first)
                 if 0 <= second < TOKENS:
                     w_inverse[second] = clamp_and_invert(w_totals[second], COLUMN_BLOCKS)

@@ -21,9 +21,12 @@ EPS = 1e-12
 
 BATCH_TILES = BATCH // P
 COLUMN_BLOCKS = FEATURES // P
+TOKEN_PAIRS = TOKENS // 2
+WORDS = HIDDEN // 2
 GROUP = 4
-GROUPS = BATCH_TILES * TOKENS // GROUP
 GROUPS_PER_TILE = TOKENS // GROUP
+GROUPS = BATCH_TILES * GROUPS_PER_TILE
+STORE_TOKENS = 2
 TILES_REGROUPED_BY_VECTOR = 2
 
 FLOPS = 2 * BATCH * TOKENS * HIDDEN * FEATURES
@@ -35,24 +38,22 @@ def tile_npertokenswishglu_basis_pb_t_kernel(tc, h, w_down_mix, out):
         ctx.enter_context(tc.manual_schedule())
         const = ctx.enter_context(tc.tile_pool(name="const", bufs=1))
         raw = ctx.enter_context(tc.tile_pool(name="raw", bufs=1))
-        keep = ctx.enter_context(tc.tile_pool(name="keep", bufs=1))
+        operands = ctx.enter_context(tc.tile_pool(name="operands", bufs=1))
         stage = ctx.enter_context(tc.tile_pool(name="stage", bufs=2))
         small = ctx.enter_context(tc.tile_pool(name="small", bufs=3))
         results = ctx.enter_context(tc.tile_pool(name="results", bufs=4))
 
         w_raw = []
         h_raw = []
-        for i in range(TOKENS):
-            w_tile = raw.tile([P, PACK, FEATURES], BF16, name="w_raw%d" % i)
+        for n in range(TOKENS):
+            w_tile = raw.tile([P, PACK, FEATURES], BF16, name="w_raw%d" % n)
             nc.sync.dma_start(
                 out=w_tile[:].rearrange("q (u e) j -> q u e j", u=2),
-                in_=w_down_mix[i].rearrange("(u q e) j -> q u e j", u=2, e=2),
+                in_=w_down_mix[n].rearrange("(u q e) j -> q u e j", u=2, e=2),
             )
             w_raw.append(w_tile)
-            h_tile = raw.tile([P, TOKENS * HIDDEN], BF16, name="h_raw%d" % i)
-            nc.sync.dma_start(
-                out=h_tile[:], in_=h[i * P : (i + 1) * P].rearrange("b l f -> b (l f)")
-            )
+            h_tile = raw.tile([P, TOKENS * HIDDEN], BF16, name="h_raw%d" % n)
+            nc.sync.dma_start(out=h_tile[:], in_=h[n * P : (n + 1) * P].rearrange("b l f -> b (l f)"))
             h_raw.append(h_tile)
 
         ident_bf16 = const.tile([P, P], BF16)
@@ -62,185 +63,190 @@ def tile_npertokenswishglu_basis_pb_t_kernel(tc, h, w_down_mix, out):
 
         one = const.tile([P, 1], F32)
         nc.vector.memset(one[:], 1.0)
-        one_root = const.tile([P, 1], F32)
-        nc.scalar.activation(out=one_root[:], in_=one[:], func=ACT.Abs_reciprocal_sqrt)
+        warm = const.tile([P, 1], F32)
+        nc.scalar.activation(out=warm[:], in_=one[:], func=ACT.Abs_reciprocal_sqrt)
 
-        w_codes = [keep.tile([P, FEATURES], U32, name="w_codes%d" % l, align_bytes=64) for l in range(TOKENS)]
-        w_scales = [keep.tile([P, FEATURES], U8, name="w_scales%d" % l, align_bytes=64) for l in range(TOKENS)]
-        h_codes = [keep.tile([P, TOKENS * P], U32, name="h_codes%d" % t, align_bytes=64) for t in range(BATCH_TILES)]
-        h_scales = [keep.tile([P, TOKENS * P], U8, name="h_scales%d" % t, align_bytes=64) for t in range(BATCH_TILES)]
+        w_codes = [operands.tile([P, FEATURES], U32, name="w_codes%d" % l, align_bytes=64) for l in range(TOKENS)]
+        w_scales = [operands.tile([P, FEATURES], U8, name="w_scales%d" % l, align_bytes=64) for l in range(TOKENS)]
+        h_codes = [operands.tile([P, TOKENS * P], U32, name="h_codes%d" % i, align_bytes=64) for i in range(BATCH_TILES)]
+        h_scales = [operands.tile([P, TOKENS * P], U8, name="h_scales%d" % i, align_bytes=64) for i in range(BATCH_TILES)]
 
         def sum_of_squares(values, total):
             squares = stage.tile([P, HIDDEN], BF16, name="squares", bufs=4)
             nc.scalar.activation(out=squares[:], in_=values, func=ACT.Square, accum_out=total)
 
-        def clamp_and_invert(totals, width):
+        def clamp(totals, width):
             clamped = small.tile([P, width], F32, name="clamped")
             nc.vector.tensor_scalar_max(out=clamped[:], in0=totals[:], scalar1=EPS * EPS)
             return clamped
 
-        def root(clamped, width):
-            scale = small.tile([P, width], F32, name="scale")
-            nc.scalar.activation(out=scale[:], in_=clamped[:], func=ACT.Abs_reciprocal_sqrt)
-            return scale
+        def inverse_root(clamped, width):
+            inverse_norm = small.tile([P, width], F32, name="inverse_norm")
+            nc.scalar.activation(out=inverse_norm[:], in_=clamped[:], func=ACT.Abs_reciprocal_sqrt)
+            return inverse_norm
 
         with tc.psum_pool(name="prep_psum", bufs=2) as prep_psum:
             w_flipped = {}
             w_totals = {}
-            w_inverse = {}
-            w_scale = {}
+            w_inverse_norm = {}
             w_spread = {}
             nd = {}
-            h_grouped = {}
             h_flipped = {}
+            h_grouped = {}
 
-            def flip_weight(i):
+            def flip_weight(l):
                 for half in range(2):
-                    w_flipped[i, half] = prep_psum.tile([P, 2, PACK, P], BF16, name="w_flipped", bufs=2)
+                    w_flipped[l, half] = prep_psum.tile([P, 2, PACK, P], BF16, name="w_flipped", bufs=2)
                     for k in range(2):
                         block = 2 * half + k
                         for t in range(PACK):
                             nc.tensor.transpose(
-                                out=w_flipped[i, half][:, k, t, :],
-                                in_=w_raw[i][:, t, block * P : (block + 1) * P],
+                                out=w_flipped[l, half][:, k, t, :],
+                                in_=w_raw[l][:, t, block * P : (block + 1) * P],
                                 identity=ident_bf16[:],
                             )
 
-            def flip_h(i):
-                h_words = h_raw[i][:].bitcast(F32)
-                for pair in range(TOKENS // 2):
-                    h_flipped[i, pair] = prep_psum.tile([P, 2, 2, P], F32, name="h_flipped", bufs=4)
-                    for k in range(2):
-                        for u in range(2):
-                            first = (2 * pair + k) * (HIDDEN // 2) + u * P
-                            nc.tensor.transpose(
-                                out=h_flipped[i, pair][:, k, u, :],
-                                in_=h_words[:, first : first + P],
-                                identity=ident_f32[:],
-                            )
+            def weight_column_sums(l):
+                w_totals[l] = small.tile([P, COLUMN_BLOCKS], F32, name="w_totals")
+                for block in range(COLUMN_BLOCKS):
+                    sum_of_squares(
+                        w_flipped[l, block // 2][:, block % 2].rearrange("j t q -> j (t q)"),
+                        w_totals[l][:, block : block + 1],
+                    )
 
-            def spread_weight_scale(i):
-                w_spread[i] = prep_psum.tile([P, FEATURES], F32, name="w_spread", bufs=2)
+            def spread_weight_norms(l):
+                w_spread[l] = prep_psum.tile([P, FEATURES], F32, name="w_spread", bufs=2)
                 for block in range(COLUMN_BLOCKS):
                     nc.tensor.matmul(
-                        out=w_spread[i][:, block * P : (block + 1) * P],
-                        lhsT=w_scale[i][:, block : block + 1].to_broadcast([P, P]),
+                        out=w_spread[l][:, block * P : (block + 1) * P],
+                        lhsT=w_inverse_norm[l][:, block : block + 1].to_broadcast([P, P]),
                         rhs=ident_f32[:],
                         start=True,
                         stop=True,
                     )
 
-            def weight_column_sums(i):
-                w_totals[i] = small.tile([P, COLUMN_BLOCKS], F32, name="w_totals")
-                for block in range(COLUMN_BLOCKS):
-                    sum_of_squares(
-                        w_flipped[i, block // 2][:, block % 2].rearrange("j t q -> j (t q)"),
-                        w_totals[i][:, block : block + 1],
-                    )
+            def normalise_weight(l):
+                nd[l] = stage.tile([P, FEATURES, PACK], BF16, name="nd", align_bytes=64)
+                nc.vector.tensor_tensor(
+                    out=nd[l][:],
+                    in0=w_raw[l][:].rearrange("q t j -> q j t"),
+                    in1=w_spread[l][:].unsqueeze(2).to_broadcast([P, FEATURES, PACK]),
+                    op=ALU.mult,
+                )
+
+            def quantise_weight(l):
+                nc.vector.quantize_mx(
+                    out=w_codes[l][:].bitcast(FP8X4),
+                    scales=w_scales[l][:],
+                    in_=nd[l][:].rearrange("q j t -> q (j t)"),
+                )
+
+            def flip_h(i):
+                h_words = h_raw[i][:].bitcast(F32)
+                for pair in range(TOKEN_PAIRS):
+                    h_flipped[i, pair] = prep_psum.tile([P, 2, 2, P], F32, name="h_flipped", bufs=4)
+                    for k in range(2):
+                        for u in range(2):
+                            start_word = (2 * pair + k) * WORDS + u * P
+                            nc.tensor.transpose(
+                                out=h_flipped[i, pair][:, k, u, :],
+                                in_=h_words[:, start_word : start_word + P],
+                                identity=ident_f32[:],
+                            )
 
             def regroup_h(i):
                 h_grouped[i] = stage.tile([P, TOKENS * P * PACK], BF16, name="h_grouped", align_bytes=64, bufs=3)
                 grouped_words = h_grouped[i][:].bitcast(F32)
                 copy = nc.vector.tensor_copy if i < TILES_REGROUPED_BY_VECTOR else nc.scalar.copy
-                for pair in range(TOKENS // 2):
+                bank_words = 2 * P * 2
+                for pair in range(TOKEN_PAIRS):
                     copy(
-                        out=grouped_words[:, pair * 512 : (pair + 1) * 512].rearrange(
+                        out=grouped_words[:, pair * bank_words : (pair + 1) * bank_words].rearrange(
                             "q (k b u) -> q k b u", k=2, u=2
                         ),
                         in_=h_flipped[i, pair][:].rearrange("q k u b -> q k b u"),
                     )
 
             def quantise_h(i):
-                for half in range(2):
+                width = GROUP * P
+                for half in range(GROUPS_PER_TILE):
                     nc.vector.quantize_mx(
-                        out=h_codes[i][:, half * 512 : (half + 1) * 512].bitcast(FP8X4),
-                        scales=h_scales[i][:, half * 512 : (half + 1) * 512],
-                        in_=h_grouped[i][:, half * 2048 : (half + 1) * 2048],
+                        out=h_codes[i][:, half * width : (half + 1) * width].bitcast(FP8X4),
+                        scales=h_scales[i][:, half * width : (half + 1) * width],
+                        in_=h_grouped[i][:, half * width * PACK : (half + 1) * width * PACK],
                     )
 
-            def normalise_weight(i):
-                nd[i] = stage.tile([P, FEATURES, PACK], BF16, name="nd", align_bytes=64)
-                nc.vector.tensor_tensor(
-                    out=nd[i][:],
-                    in0=w_raw[i][:].rearrange("q t j -> q j t"),
-                    in1=w_spread[i][:].unsqueeze(2).to_broadcast([P, FEATURES, PACK]),
-                    op=ALU.mult,
-                )
-
-            def quantise_weight(i):
-                nc.vector.quantize_mx(
-                    out=w_codes[i][:].bitcast(FP8X4),
-                    scales=w_scales[i][:],
-                    in_=nd[i][:].rearrange("q j t -> q (j t)"),
-                )
-
             for n in range(TOKENS + 2):
-                first = n
-                second = n - 1
-                third = n - 2
-                if first < TOKENS:
-                    flip_weight(first)
-                if 0 <= third:
-                    spread_weight_scale(third)
-                if first < TOKENS:
-                    flip_h(first)
-                    weight_column_sums(first)
-                if 0 <= second < TOKENS:
-                    w_inverse[second] = clamp_and_invert(w_totals[second], COLUMN_BLOCKS)
-                    w_scale[second] = root(w_inverse[second], COLUMN_BLOCKS)
-                    quantise_h(second)
-                if 0 <= third:
-                    normalise_weight(third)
-                if first < TOKENS:
-                    regroup_h(first)
-                if 0 <= third:
-                    quantise_weight(third)
+                newest = n
+                middle = n - 1
+                oldest = n - 2
+                if newest < TOKENS:
+                    flip_weight(newest)
+                if oldest >= 0:
+                    spread_weight_norms(oldest)
+                if newest < TOKENS:
+                    flip_h(newest)
+                    weight_column_sums(newest)
+                if 0 <= middle < TOKENS:
+                    w_inverse_norm[middle] = inverse_root(clamp(w_totals[middle], COLUMN_BLOCKS), COLUMN_BLOCKS)
+                    quantise_h(middle)
+                if oldest >= 0:
+                    normalise_weight(oldest)
+                if newest < TOKENS:
+                    regroup_h(newest)
+                if oldest >= 0:
+                    quantise_weight(oldest)
 
-        with tc.psum_pool(name="y_psum", bufs=8, reuse_waits="tile") as y_psum:
+        with tc.psum_pool(name="y_psum", bufs=2 * GROUP, reuse_waits="tile") as y_psum:
             y = {}
             y_totals = {}
-            y_inverse = {}
-            y_scale = {}
+            y_clamped = {}
+            y_inverse_norm = {}
             normed = {}
+
+            def multiply(g):
+                i = g // GROUPS_PER_TILE
+                for k in range(GROUP):
+                    l = (g % GROUPS_PER_TILE) * GROUP + k
+                    y[g, k] = y_psum.tile([P, FEATURES], F32, name="y")
+                    nc.tensor.matmul_mx(
+                        out=y[g, k][:],
+                        lhsT=h_codes[i][:, l * P : (l + 1) * P].bitcast(FP8X4),
+                        lhsT_scale=h_scales[i][:, l * P : (l + 1) * P],
+                        rhs=w_codes[l][:].bitcast(FP8X4),
+                        rhs_scale=w_scales[l][:],
+                        start=True,
+                        stop=True,
+                    )
+
+            def row_sum(g, k):
+                sum_of_squares(y[g, k][:], y_totals[g][:, k : k + 1])
 
             def scale_rows(g, k):
                 nc.vector.tensor_scalar_mul(
-                    out=normed[g][:, k, :], in0=y[g][k][:], scalar1=y_scale[g][:, k : k + 1]
+                    out=normed[g][:, k, :], in0=y[g, k][:], scalar1=y_inverse_norm[g][:, k : k + 1]
                 )
+                if k % STORE_TOKENS == STORE_TOKENS - 1:
+                    i = g // GROUPS_PER_TILE
+                    last_token = (g % GROUPS_PER_TILE) * GROUP + k
+                    nc.sync.dma_start(
+                        out=out[i * P : (i + 1) * P, last_token + 1 - STORE_TOKENS : last_token + 1, :],
+                        in_=normed[g][:, k + 1 - STORE_TOKENS : k + 1, :],
+                    )
 
             for g in range(GROUPS + 1):
                 if g < GROUPS:
-                    tile_index = g // GROUPS_PER_TILE
-                    y[g] = []
-                    for k in range(GROUP):
-                        l = (g % GROUPS_PER_TILE) * GROUP + k
-                        acc = y_psum.tile([P, FEATURES], F32, name="y")
-                        nc.tensor.matmul_mx(
-                            out=acc[:],
-                            lhsT=h_codes[tile_index][:, l * P : (l + 1) * P].bitcast(FP8X4),
-                            lhsT_scale=h_scales[tile_index][:, l * P : (l + 1) * P],
-                            rhs=w_codes[l][:].bitcast(FP8X4),
-                            rhs_scale=w_scales[l][:],
-                            start=True,
-                            stop=True,
-                        )
-                        y[g].append(acc)
+                    multiply(g)
                     y_totals[g] = small.tile([P, GROUP], F32, name="y_totals")
-                    sum_of_squares(y[g][0][:], y_totals[g][:, 0:1])
+                    row_sum(g, 0)
                 if g >= 1:
-                    y_scale[g - 1] = root(y_inverse[g - 1], GROUP)
+                    y_inverse_norm[g - 1] = inverse_root(y_clamped[g - 1], GROUP)
                     normed[g - 1] = results.tile([P, GROUP, FEATURES], F32, name="normed")
                     for k in range(GROUP - 1):
                         scale_rows(g - 1, k)
                 if g < GROUPS:
                     for k in range(1, GROUP):
-                        sum_of_squares(y[g][k][:], y_totals[g][:, k : k + 1])
-                    y_inverse[g] = clamp_and_invert(y_totals[g], GROUP)
+                        row_sum(g, k)
+                    y_clamped[g] = clamp(y_totals[g], GROUP)
                 if g >= 1:
                     scale_rows(g - 1, GROUP - 1)
-                    done_tile = (g - 1) // GROUPS_PER_TILE
-                    first_token = ((g - 1) % GROUPS_PER_TILE) * GROUP
-                    nc.sync.dma_start(
-                        out=out[done_tile * P : (done_tile + 1) * P, first_token : first_token + GROUP, :],
-                        in_=normed[g - 1][:],
-                    )

@@ -167,14 +167,13 @@ def tile_npertokenswishglu_basis_pb_t_kernel(tc, h, w_down_mix, out):
                         in_=h_flipped[i, pair][:].rearrange("q k u b -> q k b u"),
                     )
 
-            def quantise_h(i):
+            def quantise_h(i, half):
                 width = GROUP * P
-                for half in range(GROUPS_PER_TILE):
-                    nc.vector.quantize_mx(
-                        out=h_codes[i][:, half * width : (half + 1) * width].bitcast(FP8X4),
-                        scales=h_scales[i][:, half * width : (half + 1) * width],
-                        in_=h_grouped[i][:, half * width * PACK : (half + 1) * width * PACK],
-                    )
+                nc.vector.quantize_mx(
+                    out=h_codes[i][:, half * width : (half + 1) * width].bitcast(FP8X4),
+                    scales=h_scales[i][:, half * width : (half + 1) * width],
+                    in_=h_grouped[i][:, half * width * PACK : (half + 1) * width * PACK],
+                )
 
             for n in range(TOKENS + 2):
                 newest = n
@@ -189,9 +188,11 @@ def tile_npertokenswishglu_basis_pb_t_kernel(tc, h, w_down_mix, out):
                     weight_column_sums(newest)
                 if 0 <= middle < TOKENS:
                     w_inverse_norm[middle] = inverse_root(clamp(w_totals[middle], COLUMN_BLOCKS), COLUMN_BLOCKS)
-                    quantise_h(middle)
+                    quantise_h(middle, 0)
                 if oldest >= 0:
                     normalise_weight(oldest)
+                if 0 <= middle < TOKENS:
+                    quantise_h(middle, 1)
                 if newest < TOKENS:
                     regroup_h(newest)
                 if oldest >= 0:

from contextlib import ExitStack

import concourse.mybir as mybir
from concourse.masks import make_identity

F32 = mybir.dt.float32
BF16 = mybir.dt.bfloat16
U32 = mybir.dt.uint32
U8 = mybir.dt.uint8
FP8X4 = mybir.dt.float8_e4m3fn_x4
ACT = mybir.ActivationFunctionType
ALU = mybir.AluOpType

P = 128
BATCH = 1024
TOKENS = 8
HIDDEN = 512
FEATURES = 512
PACK = 4
EPS = 1e-12

BATCH_TILES = BATCH // P
COLUMN_BLOCKS = FEATURES // P
TOKEN_PAIRS = TOKENS // 2
WORDS = HIDDEN // 2
GROUP = 4
GROUPS_PER_TILE = TOKENS // GROUP
GROUPS = BATCH_TILES * GROUPS_PER_TILE
STORE_TOKENS = 2
TILES_REGROUPED_BY_VECTOR = 2

FLOPS = 2 * BATCH * TOKENS * HIDDEN * FEATURES


def tile_npertokenswishglu_basis_pb_t_kernel(tc, h, w_down_mix, out):
    nc = tc.nc
    with ExitStack() as ctx:
        ctx.enter_context(tc.manual_schedule())
        const = ctx.enter_context(tc.tile_pool(name="const", bufs=1))
        raw = ctx.enter_context(tc.tile_pool(name="raw", bufs=1))
        operands = ctx.enter_context(tc.tile_pool(name="operands", bufs=1))
        stage = ctx.enter_context(tc.tile_pool(name="stage", bufs=2))
        small = ctx.enter_context(tc.tile_pool(name="small", bufs=3))
        results = ctx.enter_context(tc.tile_pool(name="results", bufs=4))

        w_raw = []
        h_raw = []
        for n in range(TOKENS):
            w_tile = raw.tile([P, PACK, FEATURES], BF16, name="w_raw%d" % n)
            nc.sync.dma_start(
                out=w_tile[:].rearrange("q (u e) j -> q u e j", u=2),
                in_=w_down_mix[n].rearrange("(u q e) j -> q u e j", u=2, e=2),
            )
            w_raw.append(w_tile)
            h_tile = raw.tile([P, TOKENS * HIDDEN], BF16, name="h_raw%d" % n)
            nc.sync.dma_start(out=h_tile[:], in_=h[n * P : (n + 1) * P].rearrange("b l f -> b (l f)"))
            h_raw.append(h_tile)

        ident_bf16 = const.tile([P, P], BF16)
        make_identity(nc, ident_bf16[:])
        ident_f32 = const.tile([P, P], F32)
        make_identity(nc, ident_f32[:])

        one = const.tile([P, 1], F32)
        nc.vector.memset(one[:], 1.0)
        warm = const.tile([P, 1], F32)
        nc.scalar.activation(out=warm[:], in_=one[:], func=ACT.Abs_reciprocal_sqrt)

        w_codes = [operands.tile([P, FEATURES], U32, name="w_codes%d" % l, align_bytes=64) for l in range(TOKENS)]
        w_scales = [operands.tile([P, FEATURES], U8, name="w_scales%d" % l, align_bytes=64) for l in range(TOKENS)]
        h_codes = [operands.tile([P, TOKENS * P], U32, name="h_codes%d" % i, align_bytes=64) for i in range(BATCH_TILES)]
        h_scales = [operands.tile([P, TOKENS * P], U8, name="h_scales%d" % i, align_bytes=64) for i in range(BATCH_TILES)]

        def sum_of_squares(values, total):
            squares = stage.tile([P, HIDDEN], BF16, name="squares", bufs=4)
            nc.scalar.activation(out=squares[:], in_=values, func=ACT.Square, accum_out=total)

        def clamp(totals, width):
            clamped = small.tile([P, width], F32, name="clamped")
            nc.vector.tensor_scalar_max(out=clamped[:], in0=totals[:], scalar1=EPS * EPS)
            return clamped

        def inverse_root(clamped, width):
            inverse_norm = small.tile([P, width], F32, name="inverse_norm")
            nc.scalar.activation(out=inverse_norm[:], in_=clamped[:], func=ACT.Abs_reciprocal_sqrt)
            return inverse_norm

        with tc.psum_pool(name="prep_psum", bufs=2) as prep_psum:
            w_flipped = {}
            w_totals = {}
            w_inverse_norm = {}
            w_spread = {}
            nd = {}
            h_flipped = {}
            h_grouped = {}

            def flip_weight(l):
                for half in range(2):
                    w_flipped[l, half] = prep_psum.tile([P, 2, PACK, P], BF16, name="w_flipped", bufs=2)
                    for k in range(2):
                        block = 2 * half + k
                        for t in range(PACK):
                            nc.tensor.transpose(
                                out=w_flipped[l, half][:, k, t, :],
                                in_=w_raw[l][:, t, block * P : (block + 1) * P],
                                identity=ident_bf16[:],
                            )

            def weight_column_sums(l):
                w_totals[l] = small.tile([P, COLUMN_BLOCKS], F32, name="w_totals")
                for block in range(COLUMN_BLOCKS):
                    sum_of_squares(
                        w_flipped[l, block // 2][:, block % 2].rearrange("j t q -> j (t q)"),
                        w_totals[l][:, block : block + 1],
                    )

            def spread_weight_norms(l):
                w_spread[l] = prep_psum.tile([P, FEATURES], F32, name="w_spread", bufs=2)
                for block in range(COLUMN_BLOCKS):
                    nc.tensor.matmul(
                        out=w_spread[l][:, block * P : (block + 1) * P],
                        lhsT=w_inverse_norm[l][:, block : block + 1].to_broadcast([P, P]),
                        rhs=ident_f32[:],
                        start=True,
                        stop=True,
                    )

            def normalise_weight(l):
                nd[l] = stage.tile([P, FEATURES, PACK], BF16, name="nd", align_bytes=64)
                nc.vector.tensor_tensor(
                    out=nd[l][:],
                    in0=w_raw[l][:].rearrange("q t j -> q j t"),
                    in1=w_spread[l][:].unsqueeze(2).to_broadcast([P, FEATURES, PACK]),
                    op=ALU.mult,
                )

            def quantise_weight(l):
                nc.vector.quantize_mx(
                    out=w_codes[l][:].bitcast(FP8X4),
                    scales=w_scales[l][:],
                    in_=nd[l][:].rearrange("q j t -> q (j t)"),
                )

            def flip_h(i):
                h_words = h_raw[i][:].bitcast(F32)
                for pair in range(TOKEN_PAIRS):
                    h_flipped[i, pair] = prep_psum.tile([P, 2, 2, P], F32, name="h_flipped", bufs=4)
                    for k in range(2):
                        for u in range(2):
                            start_word = (2 * pair + k) * WORDS + u * P
                            nc.tensor.transpose(
                                out=h_flipped[i, pair][:, k, u, :],
                                in_=h_words[:, start_word : start_word + P],
                                identity=ident_f32[:],
                            )

            def regroup_h(i):
                h_grouped[i] = stage.tile([P, TOKENS * P * PACK], BF16, name="h_grouped", align_bytes=64, bufs=3)
                grouped_words = h_grouped[i][:].bitcast(F32)
                copy = nc.vector.tensor_copy if i < TILES_REGROUPED_BY_VECTOR else nc.scalar.copy
                bank_words = 2 * P * 2
                for pair in range(TOKEN_PAIRS):
                    copy(
                        out=grouped_words[:, pair * bank_words : (pair + 1) * bank_words].rearrange(
                            "q (k b u) -> q k b u", k=2, u=2
                        ),
                        in_=h_flipped[i, pair][:].rearrange("q k u b -> q k b u"),
                    )

            def quantise_h(i, half):
                width = GROUP * P
                nc.vector.quantize_mx(
                    out=h_codes[i][:, half * width : (half + 1) * width].bitcast(FP8X4),
                    scales=h_scales[i][:, half * width : (half + 1) * width],
                    in_=h_grouped[i][:, half * width * PACK : (half + 1) * width * PACK],
                )

            for n in range(TOKENS + 2):
                newest = n
                middle = n - 1
                oldest = n - 2
                if newest < TOKENS:
                    flip_weight(newest)
                if oldest >= 0:
                    spread_weight_norms(oldest)
                if newest < TOKENS:
                    flip_h(newest)
                    weight_column_sums(newest)
                if 0 <= middle < TOKENS:
                    w_inverse_norm[middle] = inverse_root(clamp(w_totals[middle], COLUMN_BLOCKS), COLUMN_BLOCKS)
                    quantise_h(middle, 0)
                if oldest >= 0:
                    normalise_weight(oldest)
                if 0 <= middle < TOKENS:
                    quantise_h(middle, 1)
                if newest < TOKENS:
                    regroup_h(newest)
                if oldest >= 0:
                    quantise_weight(oldest)

        with tc.psum_pool(name="y_psum", bufs=2 * GROUP, reuse_waits="tile") as y_psum:
            y = {}
            y_totals = {}
            y_clamped = {}
            y_inverse_norm = {}
            normed = {}

            def multiply(g):
                i = g // GROUPS_PER_TILE
                for k in range(GROUP):
                    l = (g % GROUPS_PER_TILE) * GROUP + k
                    y[g, k] = y_psum.tile([P, FEATURES], F32, name="y")
                    nc.tensor.matmul_mx(
                        out=y[g, k][:],
                        lhsT=h_codes[i][:, l * P : (l + 1) * P].bitcast(FP8X4),
                        lhsT_scale=h_scales[i][:, l * P : (l + 1) * P],
                        rhs=w_codes[l][:].bitcast(FP8X4),
                        rhs_scale=w_scales[l][:],
                        start=True,
                        stop=True,
                    )

            def row_sum(g, k):
                sum_of_squares(y[g, k][:], y_totals[g][:, k : k + 1])

            def scale_rows(g, k):
                nc.vector.tensor_scalar_mul(
                    out=normed[g][:, k, :], in0=y[g, k][:], scalar1=y_inverse_norm[g][:, k : k + 1]
                )
                if k % STORE_TOKENS == STORE_TOKENS - 1:
                    i = g // GROUPS_PER_TILE
                    last_token = (g % GROUPS_PER_TILE) * GROUP + k
                    nc.sync.dma_start(
                        out=out[i * P : (i + 1) * P, last_token + 1 - STORE_TOKENS : last_token + 1, :],
                        in_=normed[g][:, k + 1 - STORE_TOKENS : k + 1, :],
                    )

            for g in range(GROUPS + 1):
                if g < GROUPS:
                    multiply(g)
                    y_totals[g] = small.tile([P, GROUP], F32, name="y_totals")
                    row_sum(g, 0)
                if g >= 1:
                    y_inverse_norm[g - 1] = inverse_root(y_clamped[g - 1], GROUP)
                    normed[g - 1] = results.tile([P, GROUP, FEATURES], F32, name="normed")
                    for k in range(GROUP - 1):
                        scale_rows(g - 1, k)
                if g < GROUPS:
                    for k in range(1, GROUP):
                        row_sum(g, k)
                    y_clamped[g] = clamp(y_totals[g], GROUP)
                if g >= 1:
                    scale_rows(g - 1, GROUP - 1)
